import numpy as np
import ml_dtypes


def mxq(x, axis, fmt="e4m3"):
    dtype, down = {"e4m3": (ml_dtypes.float8_e4m3fn, 7), "e5m2": (ml_dtypes.float8_e5m2, 14)}[fmt]
    v = np.moveaxis(np.asarray(x, np.float32).astype(ml_dtypes.bfloat16).astype(np.float64), axis, -1)
    blocks = v.reshape(v.shape[:-1] + (-1, 32))
    amax = np.abs(blocks).max(-1, keepdims=True)
    byte = np.maximum(np.where(amax > 0, np.frexp(amax)[1] - 1 + 127, 0) - down, 1)
    scale = np.exp2(byte - 127.0)
    codes = (blocks / scale).astype(np.float32).astype(dtype).astype(np.float64)
    return np.moveaxis((codes * scale).reshape(v.shape), -1, axis)


WIDE = False


def mx_kscale(k):
    if not WIDE:
        return np.ones(k)
    levels = np.array([10, -10, 5, -5, 0])
    a = np.random.permutation(np.resize(levels, k // 512 * 4)).reshape(k // 512, 4)
    idx = np.arange(k)
    return np.exp2(a[idx // 512, idx % 128 // 32])


BF16 = ml_dtypes.bfloat16


def bf(x):
    return np.asarray(x, np.float32).astype(BF16)


def f64(x):
    return np.asarray(x).astype(np.float64)


B, C, T, V, S = 4, 64, 16, 256, 4
O = C
K = S * V
EPS = 1e-5
ZS = 0.35


def setup_inputs():
    s = mx_kscale(K).reshape(S, V)
    z = (np.random.standard_normal((S, B, O, T, V)) + np.random.standard_normal(O)[None, None, :, None, None] / np.sqrt(K)) * ZS
    return {"z": bf(z * s[:, None, None, None, :]),
            "A": bf(np.random.uniform(size=(S, V, V)) / s[:, :, None]),
            "x": bf(np.random.standard_normal((B, C, T, V))),
            "gamma": bf(1.0 + 0.1 * np.random.standard_normal(O)),
            "beta": bf(0.1 * np.random.standard_normal(O))}


def reference(z, A, x, gamma, beta):
    x = f64(x)
    zk = np.moveaxis(f64(z), 0, 3).reshape(B, O, T, K)
    ak = f64(A).reshape(K, V)
    y = mxq(zk, 3, "e4m3") @ mxq(ak, 0, "e4m3")
    mean = y.mean(axis=(0, 2, 3), keepdims=True)
    var = y.var(axis=(0, 2, 3), keepdims=True)
    y_hat = (y - mean) / np.sqrt(var + EPS)
    y_bn = y_hat * f64(gamma)[None, :, None, None] + f64(beta)[None, :, None, None]
    return np.maximum(y_bn + x, 0.0)

@@ -1,0 +1,211 @@
+from contextlib import ExitStack
+
+import concourse.bass as bass
+import concourse.mybir as mybir
+import concourse.tile as tile
+from concourse.masks import make_identity
+
+FP8X4 = mybir.dt.float8_e4m3fn_x4
+BF16 = mybir.dt.bfloat16
+F32 = mybir.dt.float32
+U32 = mybir.dt.uint32
+U8 = mybir.dt.uint8
+ALU = mybir.AluOpType
+ACT = mybir.ActivationFunctionType
+
+S, B, O, T, V = 4, 4, 64, 16, 256
+P = 128
+EPS = 1e-5
+FLOPS = 2 * B * O * T * S * V * V
+NQ = 8
+PIN = True
+
+
+def tile_dggcn_sparse_assemble_pa_kernel(tc, z, A, x, gamma, beta, out):
+    nc = tc.nc
+    with ExitStack() as ctx:
+        if PIN:
+            ctx.enter_context(tc.manual_schedule())
+        const = ctx.enter_context(tc.tile_pool(name="const", bufs=1))
+        keep = ctx.enter_context(tc.tile_pool(name="keep", bufs=1))
+        gpool = ctx.enter_context(tc.tile_pool(name="gpool", bufs=4))
+        tpool = ctx.enter_context(tc.tile_pool(name="tpool", bufs=4))
+        psum = ctx.enter_context(tc.psum_pool(name="psum", bufs=1))
+
+        zv = z.rearrange("s b o (th tl) v -> b (o th) s (tl v)", th=2)
+        xv = x.rearrange("b c (th tl) v -> b (c th) (tl v)", th=2)
+        ov = out.rearrange("b c (th tl) v -> b (c th) (tl v)", th=2)
+        av = A.rearrange("s (q e) w -> q s (e w)", e=2)
+
+        chunks = [2, 2] + [4] * (NQ - 1)
+        zch = [keep.tile([P, S, n * V], BF16, name="zch%d" % c) for c, n in enumerate(chunks)]
+        zsrc = []
+        for c, n in enumerate(chunks):
+            for k in range(n):
+                zsrc.append((c, k))
+        araw = const.tile([P, 2 * S, V], BF16, name="araw")
+        xs = [keep.tile([P, 2048], BF16, name="xs%d" % b) for b in range(B)]
+
+        def load_z(c):
+            i0 = sum(chunks[:c])
+            c0 = (i0 % 8) * V
+            nc.sync.dma_start(out=zch[c][:], in_=zv[i0 // 8, :, :, c0:c0 + chunks[c] * V])
+
+        load_z(0)
+        nc.sync.dma_start(out=araw[:].rearrange("q (s e) w -> q s (e w)", e=2), in_=av)
+        for c in range(1, len(chunks)):
+            load_z(c)
+        for b in (3, 0, 1, 2):
+            nc.sync.dma_start(out=xs[b][:], in_=xv[b])
+
+        ident = const.tile([P, P], F32, name="ident")
+        make_identity(nc, ident[:])
+        gb_rows = const.tile([P, 2 * O], BF16, name="gb_rows")
+        nc.vector.memset(gb_rows[:], 0.0)
+        nc.scalar.dma_start(out=gb_rows[0:1, 0:O], in_=gamma.rearrange("(u o) -> u o", u=1))
+        nc.scalar.dma_start(out=gb_rows[1:2, O:2 * O], in_=beta.rearrange("(u o) -> u o", u=1))
+
+        one = const.tile([P, 1], F32, name="one")
+        nc.vector.memset(one[:], 1.0)
+        warm = const.tile([P, 1], F32, name="warm")
+        nc.scalar.activation(out=warm[:], in_=one[:], func=ACT.Sqrt)
+        eps_t = const.tile([P, 1], F32, name="eps_t")
+        nc.vector.memset(eps_t[:], EPS)
+
+        idv = ident[:].rearrange("p (o r) -> p o r", r=2)
+        half = const.tile([P, O], F32, name="half")
+        nc.vector.tensor_tensor(out=half[:], in0=idv[:, :, 0], in1=idv[:, :, 1], op=ALU.add)
+        pair = const.tile([P, O, 2], F32, name="pair")
+        nc.vector.tensor_scalar(out=pair[:], in0=half[:].unsqueeze(2).to_broadcast([P, O, 2]),
+                                scalar1=0.5, scalar2=None, op0=ALU.mult)
+
+        gb_wide = const.tile([P, O, 2], F32, name="gb_wide")
+        nc.vector.tensor_tensor(out=gb_wide[:], in0=gb_rows[:, 0:O].unsqueeze(2).to_broadcast([P, O, 2]),
+                                in1=gb_rows[:, O:2 * O].unsqueeze(2).to_broadcast([P, O, 2]), op=ALU.add)
+        gb_ps = psum.tile([P, 2], F32, name="gb_ps", tag="bank7")
+        nc.tensor.matmul(out=gb_ps[:], lhsT=gb_wide[:].rearrange("p o r -> p (o r)"), rhs=ident[:, 0:2],
+                         start=True, stop=True)
+
+        agr = const.tile([P, 2, V, 4], BF16, name="agr", align_bytes=64)
+        for g in range(2):
+            nc.vector.tensor_copy(out=agr[:, g], in_=araw[:, 4 * g:4 * g + 4, :].rearrange("q t w -> q w t"))
+        a_codes = const.tile([P, 2 * V], U32, name="a_codes", align_bytes=64)
+        a_scales = const.tile([P, 2 * V], U8, name="a_scales", align_bytes=64)
+        nc.vector.quantize_mx(out=a_codes[:].bitcast(FP8X4), scales=a_scales[:],
+                              in_=agr[:].rearrange("q g w t -> q (g w t)"))
+
+        gn = const.tile([P, 2], F32, name="gn")
+        nc.vector.tensor_copy(out=gn[:, 0:1], in_=gb_ps[:, 0:1])
+        nc.vector.tensor_scalar(out=gn[:, 1:2], in0=gb_ps[:, 0:1], scalar1=-1.0, scalar2=None, op0=ALU.mult)
+        beta_f = const.tile([P, 1], F32, name="beta_f")
+        nc.vector.tensor_copy(out=beta_f[:], in_=gb_ps[:, 1:2])
+
+        z_codes = [keep.tile([P, 512], U32, name="z_codes%d" % j, align_bytes=64) for j in range(2 * NQ)]
+        z_scales = [keep.tile([P, 512], U8, name="z_scales%d" % j, align_bytes=64) for j in range(2 * NQ)]
+        stats = const.tile([P, 2 * NQ, 6], F32, name="stats")
+
+        xts = {}
+        grp = {}
+        ybank = {}
+
+        def transposes(q):
+            for i in range(4):
+                c, k = zsrc[4 * q + i]
+                zf = zch[c][:].bitcast(F32)
+                xt = psum.tile([P, S, P], F32, name="xt%d_%d" % (q, i), tag="bank%d" % i)
+                for s in range(S):
+                    nc.tensor.transpose(xt[:, s, :], zf[:, s, k * P:(k + 1) * P], ident[:])
+                xts[(q, i)] = xt
+
+        def evacuate(q):
+            for a in range(2):
+                gt = gpool.tile([P, 2, 2, P, 4], BF16, name="gt%d_%d" % (q, a), tag="gt", align_bytes=64)
+                for i2 in range(2):
+                    nc.scalar.copy(out=gt[:, i2].bitcast(F32),
+                                   in_=xts[(q, 2 * a + i2)][:].rearrange("q (g u) r -> q g r u", u=2))
+                grp[2 * q + a] = gt
+
+        def quantise(j):
+            nc.vector.quantize_mx(out=z_codes[j][:].bitcast(FP8X4), scales=z_scales[j][:],
+                                  in_=grp[j][:].rearrange("q i g r t -> q (i g r t)"))
+
+        def multiply(j, bank):
+            yb = psum.tile([P, 512], F32, name="yb%d_%d" % (j, bank), tag="bank%d" % bank)
+            for i2 in range(2):
+                for g in range(2):
+                    c0 = (2 * i2 + g) * P
+                    nc.tensor.matmul_mx(out=yb[:, i2 * V:(i2 + 1) * V],
+                                        lhsT=z_codes[j][:, c0:c0 + P].bitcast(FP8X4),
+                                        lhsT_scale=z_scales[j][:, c0:c0 + P],
+                                        rhs=a_codes[:, g * V:(g + 1) * V].bitcast(FP8X4),
+                                        rhs_scale=a_scales[:, g * V:(g + 1) * V],
+                                        start=(g == 0), stop=(g == 1))
+            ybank[j] = yb
+
+        def statistics(j):
+            nc.vector.bn_stats(out=stats[:, j, :], in_=ybank[j][:])
+
+        transposes(0)
+        evacuate(0)
+        quantise(0)
+        quantise(1)
+        for q in range(1, NQ + 1):
+            if q < NQ:
+                transposes(q)
+            for a in range(2):
+                multiply(2 * (q - 1) + a, 4 + 2 * ((q - 1) % 2) + a)
+            if q < NQ:
+                evacuate(q)
+                quantise(2 * q)
+            statistics(2 * (q - 1))
+            if q < NQ:
+                quantise(2 * q + 1)
+            statistics(2 * (q - 1) + 1)
+
+        multiply(0, 0)
+        multiply(1, 1)
+
+        mom = const.tile([P, 2], F32, name="mom")
+        nc.vector.bn_aggr(out=mom[:], in_=stats[:].rearrange("p j k -> p (j k)"))
+        nc.vector.scalar_tensor_tensor(out=mom[:, 1:2], in0=mom[:, 0:1], scalar=mom[:, 0:1], in1=mom[:, 1:2],
+                                       op0=ALU.mult, op1=ALU.add)
+        mom_ps = psum.tile([P, 2], F32, name="mom_ps", tag="bank3")
+        nc.tensor.matmul(out=mom_ps[:], lhsT=pair[:].rearrange("p o r -> p (o r)"), rhs=mom[:], start=True, stop=True)
+        ch = const.tile([P, 2], F32, name="ch")
+        nc.vector.tensor_copy(out=ch[:], in_=mom_ps[:])
+        negvar = const.tile([P, 1], F32, name="negvar")
+        nc.vector.scalar_tensor_tensor(out=negvar[:], in0=ch[:, 0:1], scalar=ch[:, 0:1], in1=ch[:, 1:2],
+                                       op0=ALU.mult, op1=ALU.subtract)
+        std = const.tile([P, 1], F32, name="std")
+        nc.scalar.activation(out=std[:], in_=negvar[:], func=ACT.Sqrt, bias=eps_t[:, 0:1], scale=-1.0)
+        rstd = const.tile([P, 1], F32, name="rstd")
+        nc.vector.reciprocal(out=rstd[:], in_=std[:])
+        sc2 = const.tile([P, 2], F32, name="sc2")
+        nc.vector.tensor_scalar(out=sc2[:], in0=gn[:], scalar1=rstd[:, 0:1], scalar2=None, op0=ALU.mult)
+        shift = const.tile([P, 1], F32, name="shift")
+        nc.vector.scalar_tensor_tensor(out=shift[:], in0=ch[:, 0:1], scalar=sc2[:, 1:2], in1=beta_f[:],
+                                       op0=ALU.mult, op1=ALU.add)
+
+        multiply(2, 2)
+        multiply(3, 3)
+
+        order = [12, 13, 14, 15] + list(range(12))
+        banks = [4, 5, 6, 7, 0, 1, 2, 3]
+        res = {}
+        for n in range(16):
+            j = order[n]
+            b = j // 4
+            c0 = (j % 4) * 512
+            hq = j % 2
+            if hq == 0:
+                res[j // 2] = tpool.tile([P, 1024], F32, name="res%d" % (j // 2), tag="res")
+            rt = res[j // 2]
+            nc.vector.scalar_tensor_tensor(out=rt[:, hq * 512:(hq + 1) * 512], in0=ybank[j][:], scalar=sc2[:, 0:1],
+                                           in1=xs[b][:, c0:c0 + 512], op0=ALU.mult, op1=ALU.add)
+            nc.scalar.activation(out=rt[:, hq * 512:(hq + 1) * 512], in_=rt[:, hq * 512:(hq + 1) * 512],
+                                 func=ACT.Relu, bias=shift[:, 0:1], scale=1.0)
+            if hq == 1:
+                q0 = ((j % 4) // 2) * 1024
+                nc.sync.dma_start(out=ov[b, :, q0:q0 + 1024], in_=rt[:])
+            if n + 8 < 16:
+                multiply(order[n + 8], banks[n % 8])

@@ -79,13 +79,6 @@ def tile_dggcn_sparse_assemble_pa_kernel(tc, z, A, x, gamma, beta, out):
         nc.vector.tensor_scalar(out=pair[:], in0=half[:].unsqueeze(2).to_broadcast([P, O, 2]),
                                 scalar1=0.5, scalar2=None, op0=ALU.mult)
 
-        gb_wide = const.tile([P, O, 2], F32, name="gb_wide")
-        nc.vector.tensor_tensor(out=gb_wide[:], in0=gb_rows[:, 0:O].unsqueeze(2).to_broadcast([P, O, 2]),
-                                in1=gb_rows[:, O:2 * O].unsqueeze(2).to_broadcast([P, O, 2]), op=ALU.add)
-        gb_ps = psum.tile([P, 2], F32, name="gb_ps", tag="bank7")
-        nc.tensor.matmul(out=gb_ps[:], lhsT=gb_wide[:].rearrange("p o r -> p (o r)"), rhs=ident[:, 0:2],
-                         start=True, stop=True)
-
         agr = const.tile([P, 2, V, 4], BF16, name="agr", align_bytes=64)
         for g in range(2):
             nc.vector.tensor_copy(out=agr[:, g], in_=araw[:, 4 * g:4 * g + 4, :].rearrange("q t w -> q w t"))
@@ -94,15 +87,36 @@ def tile_dggcn_sparse_assemble_pa_kernel(tc, z, A, x, gamma, beta, out):
         nc.vector.quantize_mx(out=a_codes[:].bitcast(FP8X4), scales=a_scales[:],
                               in_=agr[:].rearrange("q g w t -> q (g w t)"))
 
+        gb_wide = const.tile([P, O, 2], F32, name="gb_wide")
         gn = const.tile([P, 2], F32, name="gn")
-        nc.vector.tensor_copy(out=gn[:, 0:1], in_=gb_ps[:, 0:1])
-        nc.vector.tensor_scalar(out=gn[:, 1:2], in0=gb_ps[:, 0:1], scalar1=-1.0, scalar2=None, op0=ALU.mult)
         beta_f = const.tile([P, 1], F32, name="beta_f")
-        nc.vector.tensor_copy(out=beta_f[:], in_=gb_ps[:, 1:2])
+        gbp = {}
+
+        def spread_gb_vector():
+            nc.vector.tensor_tensor(out=gb_wide[:], in0=gb_rows[:, 0:O].unsqueeze(2).to_broadcast([P, O, 2]),
+                                    in1=gb_rows[:, O:2 * O].unsqueeze(2).to_broadcast([P, O, 2]), op=ALU.add)
+
+        def spread_gb_tensor(bank):
+            gb_ps = psum.tile([P, 2], F32, name="gb_ps", tag="bank%d" % bank)
+            nc.tensor.matmul(out=gb_ps[:], lhsT=gb_wide[:].rearrange("p o r -> p (o r)"), rhs=ident[:, 0:2],
+                             start=True, stop=True)
+            gbp[0] = gb_ps
+
+        def spread_gb_out():
+            gb_ps = gbp[0]
+            nc.vector.tensor_copy(out=gn[:, 0:1], in_=gb_ps[:, 0:1])
+            nc.vector.tensor_scalar(out=gn[:, 1:2], in0=gb_ps[:, 0:1], scalar1=-1.0, scalar2=None, op0=ALU.mult)
+            nc.vector.tensor_copy(out=beta_f[:], in_=gb_ps[:, 1:2])
 
         z_codes = [keep.tile([P, 512], U32, name="z_codes%d" % j, align_bytes=64) for j in range(2 * NQ)]
         z_scales = [keep.tile([P, 512], U8, name="z_scales%d" % j, align_bytes=64) for j in range(2 * NQ)]
-        stats = const.tile([P, 2 * NQ, 6], F32, name="stats")
+        NE = 2 * NQ - 2
+        stats = const.tile([P, NE, 6], F32, name="stats")
+        late = const.tile([P, 15], F32, name="late")
+        nc.vector.memset(late[:, 0:1], float(NE * 512))
+        weight = const.tile([P, 2], F32, name="weight")
+        nc.vector.memset(weight[:, 0:1], 1.0)
+        nc.vector.memset(weight[:, 1:2], float(NE * 512))
 
         xts = {}
         grp = {}
@@ -143,7 +157,10 @@ def tile_dggcn_sparse_assemble_pa_kernel(tc, z, A, x, gamma, beta, out):
             ybank[j] = yb
 
         def statistics(j):
-            nc.vector.bn_stats(out=stats[:, j, :], in_=ybank[j][:])
+            if j < NE:
+                nc.vector.bn_stats(out=stats[:, j, :], in_=ybank[j][:])
+            else:
+                nc.vector.bn_stats(out=late[:, 3 + 6 * (j - NE):9 + 6 * (j - NE)], in_=ybank[j][:])
 
         transposes(0)
         evacuate(0)
@@ -154,28 +171,36 @@ def tile_dggcn_sparse_assemble_pa_kernel(tc, z, A, x, gamma, beta, out):
                 transposes(q)
             for a in range(2):
                 multiply(2 * (q - 1) + a, 4 + 2 * ((q - 1) % 2) + a)
+            if q == 4:
+                spread_gb_tensor(4)
             if q < NQ:
                 evacuate(q)
                 quantise(2 * q)
+            else:
+                early = const.tile([P, 2], F32, name="early")
+                nc.vector.bn_aggr(out=early[:], in_=stats[:].rearrange("p j k -> p (j k)"))
+                nc.vector.tensor_tensor(out=late[:, 1:3], in0=early[:], in1=weight[:], op=ALU.mult)
             statistics(2 * (q - 1))
+            statistics(2 * (q - 1) + 1)
             if q < NQ:
                 quantise(2 * q + 1)
-            statistics(2 * (q - 1) + 1)
+            if q == 3:
+                spread_gb_vector()
+            if q == 4:
+                spread_gb_out()
 
         multiply(0, 0)
         multiply(1, 1)
 
         mom = const.tile([P, 2], F32, name="mom")
-        nc.vector.bn_aggr(out=mom[:], in_=stats[:].rearrange("p j k -> p (j k)"))
+        nc.vector.bn_aggr(out=mom[:], in_=late[:])
         nc.vector.scalar_tensor_tensor(out=mom[:, 1:2], in0=mom[:, 0:1], scalar=mom[:, 0:1], in1=mom[:, 1:2],
                                        op0=ALU.mult, op1=ALU.add)
         mom_ps = psum.tile([P, 2], F32, name="mom_ps", tag="bank3")
         nc.tensor.matmul(out=mom_ps[:], lhsT=pair[:].rearrange("p o r -> p (o r)"), rhs=mom[:], start=True, stop=True)
-        ch = const.tile([P, 2], F32, name="ch")
-        nc.vector.tensor_copy(out=ch[:], in_=mom_ps[:])
         negvar = const.tile([P, 1], F32, name="negvar")
-        nc.vector.scalar_tensor_tensor(out=negvar[:], in0=ch[:, 0:1], scalar=ch[:, 0:1], in1=ch[:, 1:2],
-                                       op0=ALU.mult, op1=ALU.subtract)
+        nc.vector.tensor_scalar(out=negvar[:], in0=mom_ps[:, 0:1], scalar1=mom_ps[:, 0:1], scalar2=mom_ps[:, 1:2],
+                                op0=ALU.mult, op1=ALU.subtract)
         std = const.tile([P, 1], F32, name="std")
         nc.scalar.activation(out=std[:], in_=negvar[:], func=ACT.Sqrt, bias=eps_t[:, 0:1], scale=-1.0)
         rstd = const.tile([P, 1], F32, name="rstd")
@@ -183,7 +208,7 @@ def tile_dggcn_sparse_assemble_pa_kernel(tc, z, A, x, gamma, beta, out):
         sc2 = const.tile([P, 2], F32, name="sc2")
         nc.vector.tensor_scalar(out=sc2[:], in0=gn[:], scalar1=rstd[:, 0:1], scalar2=None, op0=ALU.mult)
         shift = const.tile([P, 1], F32, name="shift")
-        nc.vector.scalar_tensor_tensor(out=shift[:], in0=ch[:, 0:1], scalar=sc2[:, 1:2], in1=beta_f[:],
+        nc.vector.scalar_tensor_tensor(out=shift[:], in0=mom_ps[:, 0:1], scalar=sc2[:, 1:2], in1=beta_f[:],
                                        op0=ALU.mult, op1=ALU.add)
 
         multiply(2, 2)
@@ -202,9 +227,8 @@ def tile_dggcn_sparse_assemble_pa_kernel(tc, z, A, x, gamma, beta, out):
             rt = res[j // 2]
             nc.vector.scalar_tensor_tensor(out=rt[:, hq * 512:(hq + 1) * 512], in0=ybank[j][:], scalar=sc2[:, 0:1],
                                            in1=xs[b][:, c0:c0 + 512], op0=ALU.mult, op1=ALU.add)
-            nc.scalar.activation(out=rt[:, hq * 512:(hq + 1) * 512], in_=rt[:, hq * 512:(hq + 1) * 512],
-                                 func=ACT.Relu, bias=shift[:, 0:1], scale=1.0)
             if hq == 1:
+                nc.scalar.activation(out=rt[:], in_=rt[:], func=ACT.Relu, bias=shift[:, 0:1], scale=1.0)
                 q0 = ((j % 4) // 2) * 1024
                 nc.sync.dma_start(out=ov[b, :, q0:q0 + 1024], in_=rt[:])
             if n + 8 < 16:

@@ -1,8 +1,6 @@
 from contextlib import ExitStack
 
-import concourse.bass as bass
 import concourse.mybir as mybir
-import concourse.tile as tile
 from concourse.masks import make_identity
 
 FP8X4 = mybir.dt.float8_e4m3fn_x4
@@ -17,7 +15,13 @@ S, B, O, T, V = 4, 4, 64, 16, 256
 P = 128
 EPS = 1e-5
 FLOPS = 2 * B * O * T * S * V * V
-NQ = 8
+
+TILES = B * O * T // P
+PAIRS = TILES // 2
+GROUP = 4
+T_BANKS = GROUP
+Y_BANKS = 7 - GROUP
+MISC_BANK = 7
 PIN = True
 
 
@@ -28,8 +32,8 @@ def tile_dggcn_sparse_assemble_pa_kernel(tc, z, A, x, gamma, beta, out):
             ctx.enter_context(tc.manual_schedule())
         const = ctx.enter_context(tc.tile_pool(name="const", bufs=1))
         keep = ctx.enter_context(tc.tile_pool(name="keep", bufs=1))
-        gpool = ctx.enter_context(tc.tile_pool(name="gpool", bufs=4))
-        tpool = ctx.enter_context(tc.tile_pool(name="tpool", bufs=4))
+        gpool = ctx.enter_context(tc.tile_pool(name="gpool", bufs=8))
+        rpool = ctx.enter_context(tc.tile_pool(name="rpool", bufs=4))
         psum = ctx.enter_context(tc.psum_pool(name="psum", bufs=1))
 
         zv = z.rearrange("s b o (th tl) v -> b (o th) s (tl v)", th=2)
@@ -37,167 +41,161 @@ def tile_dggcn_sparse_assemble_pa_kernel(tc, z, A, x, gamma, beta, out):
         ov = out.rearrange("b c (th tl) v -> b (c th) (tl v)", th=2)
         av = A.rearrange("s (q e) w -> q s (e w)", e=2)
 
-        chunks = [2, 2] + [4] * (NQ - 1)
-        zch = [keep.tile([P, S, n * V], BF16, name="zch%d" % c) for c, n in enumerate(chunks)]
-        zsrc = []
-        for c, n in enumerate(chunks):
-            for k in range(n):
-                zsrc.append((c, k))
-        araw = const.tile([P, 2 * S, V], BF16, name="araw")
-        xs = [keep.tile([P, 2048], BF16, name="xs%d" % b) for b in range(B)]
-
-        def load_z(c):
-            i0 = sum(chunks[:c])
-            c0 = (i0 % 8) * V
-            nc.sync.dma_start(out=zch[c][:], in_=zv[i0 // 8, :, :, c0:c0 + chunks[c] * V])
-
-        load_z(0)
-        nc.sync.dma_start(out=araw[:].rearrange("q (s e) w -> q s (e w)", e=2), in_=av)
-        for c in range(1, len(chunks)):
-            load_z(c)
-        for b in (3, 0, 1, 2):
-            nc.sync.dma_start(out=xs[b][:], in_=xv[b])
-
-        ident = const.tile([P, P], F32, name="ident")
-        make_identity(nc, ident[:])
         gb_rows = const.tile([P, 2 * O], BF16, name="gb_rows")
         nc.vector.memset(gb_rows[:], 0.0)
         nc.scalar.dma_start(out=gb_rows[0:1, 0:O], in_=gamma.rearrange("(u o) -> u o", u=1))
         nc.scalar.dma_start(out=gb_rows[1:2, O:2 * O], in_=beta.rearrange("(u o) -> u o", u=1))
 
+        chunks = [2, 2] + [4] * (TILES // 4 - 1)
+        z_raw = [keep.tile([P, S, n * V], BF16, name="z_raw%d" % c) for c, n in enumerate(chunks)]
+        where = [(c, k) for c, n in enumerate(chunks) for k in range(n)]
+        a_raw = const.tile([P, 2 * S, V], BF16, name="a_raw")
+        x_sb = [keep.tile([P, 8 * V], BF16, name="x_sb%d" % b) for b in range(B)]
+
+        def load_z(c):
+            t0 = sum(chunks[:c])
+            c0 = (t0 % 8) * V
+            nc.sync.dma_start(out=z_raw[c][:], in_=zv[t0 // 8, :, :, c0:c0 + chunks[c] * V])
+
+        load_z(0)
+        nc.sync.dma_start(out=a_raw[:].rearrange("q (s e) w -> q s (e w)", e=2), in_=av)
+        for c in range(1, len(chunks)):
+            load_z(c)
+        for b in (3, 0, 1, 2):
+            nc.sync.dma_start(out=x_sb[b][:], in_=xv[b])
+
+        ident = const.tile([P, P], F32, name="ident")
+        make_identity(nc, ident[:])
         one = const.tile([P, 1], F32, name="one")
         nc.vector.memset(one[:], 1.0)
         warm = const.tile([P, 1], F32, name="warm")
         nc.scalar.activation(out=warm[:], in_=one[:], func=ACT.Sqrt)
         eps_t = const.tile([P, 1], F32, name="eps_t")
         nc.vector.memset(eps_t[:], EPS)
-
         idv = ident[:].rearrange("p (o r) -> p o r", r=2)
         half = const.tile([P, O], F32, name="half")
         nc.vector.tensor_tensor(out=half[:], in0=idv[:, :, 0], in1=idv[:, :, 1], op=ALU.add)
-        pair = const.tile([P, O, 2], F32, name="pair")
-        nc.vector.tensor_scalar(out=pair[:], in0=half[:].unsqueeze(2).to_broadcast([P, O, 2]),
+        pair_avg = const.tile([P, O, 2], F32, name="pair_avg")
+        nc.vector.tensor_scalar(out=pair_avg[:], in0=half[:].unsqueeze(2).to_broadcast([P, O, 2]),
                                 scalar1=0.5, scalar2=None, op0=ALU.mult)
 
-        agr = const.tile([P, 2, V, 4], BF16, name="agr", align_bytes=64)
+        a_grp = const.tile([P, 2, V, 4], BF16, name="a_grp", align_bytes=64)
         for g in range(2):
-            nc.vector.tensor_copy(out=agr[:, g], in_=araw[:, 4 * g:4 * g + 4, :].rearrange("q t w -> q w t"))
+            nc.vector.tensor_copy(out=a_grp[:, g], in_=a_raw[:, 4 * g:4 * g + 4, :].rearrange("q t w -> q w t"))
         a_codes = const.tile([P, 2 * V], U32, name="a_codes", align_bytes=64)
         a_scales = const.tile([P, 2 * V], U8, name="a_scales", align_bytes=64)
         nc.vector.quantize_mx(out=a_codes[:].bitcast(FP8X4), scales=a_scales[:],
-                              in_=agr[:].rearrange("q g w t -> q (g w t)"))
+                              in_=a_grp[:].rearrange("q g w t -> q (g w t)"))
 
         gb_wide = const.tile([P, O, 2], F32, name="gb_wide")
-        gn = const.tile([P, 2], F32, name="gn")
+        gamma_pm = const.tile([P, 2], F32, name="gamma_pm")
         beta_f = const.tile([P, 1], F32, name="beta_f")
-        gbp = {}
+        gb_ps = psum.tile([P, 2], F32, name="gb_ps", tag="bank%d" % MISC_BANK)
 
-        def spread_gb_vector():
+        def spread_rows():
             nc.vector.tensor_tensor(out=gb_wide[:], in0=gb_rows[:, 0:O].unsqueeze(2).to_broadcast([P, O, 2]),
                                     in1=gb_rows[:, O:2 * O].unsqueeze(2).to_broadcast([P, O, 2]), op=ALU.add)
 
-        def spread_gb_tensor(bank):
-            gb_ps = psum.tile([P, 2], F32, name="gb_ps", tag="bank%d" % bank)
+        def spread_matmul():
             nc.tensor.matmul(out=gb_ps[:], lhsT=gb_wide[:].rearrange("p o r -> p (o r)"), rhs=ident[:, 0:2],
                              start=True, stop=True)
-            gbp[0] = gb_ps
 
-        def spread_gb_out():
-            gb_ps = gbp[0]
-            nc.vector.tensor_copy(out=gn[:, 0:1], in_=gb_ps[:, 0:1])
-            nc.vector.tensor_scalar(out=gn[:, 1:2], in0=gb_ps[:, 0:1], scalar1=-1.0, scalar2=None, op0=ALU.mult)
+        def spread_out():
+            nc.vector.tensor_copy(out=gamma_pm[:, 0:1], in_=gb_ps[:, 0:1])
+            nc.vector.tensor_scalar(out=gamma_pm[:, 1:2], in0=gb_ps[:, 0:1], scalar1=-1.0, scalar2=None, op0=ALU.mult)
             nc.vector.tensor_copy(out=beta_f[:], in_=gb_ps[:, 1:2])
 
-        z_codes = [keep.tile([P, 512], U32, name="z_codes%d" % j, align_bytes=64) for j in range(2 * NQ)]
-        z_scales = [keep.tile([P, 512], U8, name="z_scales%d" % j, align_bytes=64) for j in range(2 * NQ)]
-        NE = 2 * NQ - 2
-        stats = const.tile([P, NE, 6], F32, name="stats")
-        late = const.tile([P, 15], F32, name="late")
-        nc.vector.memset(late[:, 0:1], float(NE * 512))
-        weight = const.tile([P, 2], F32, name="weight")
-        nc.vector.memset(weight[:, 0:1], 1.0)
-        nc.vector.memset(weight[:, 1:2], float(NE * 512))
+        z_codes = [keep.tile([P, 2 * P], U32, name="z_codes%d" % t, align_bytes=64) for t in range(TILES)]
+        z_scales = [keep.tile([P, 2 * P], U8, name="z_scales%d" % t, align_bytes=64) for t in range(TILES)]
+        stats = const.tile([P, PAIRS, 6], F32, name="stats")
+        turned = {}
+        grouped = {}
+        y_ps = {}
+        bank_of = {}
 
-        xts = {}
-        grp = {}
-        ybank = {}
+        def transposes(t):
+            c, k = where[t]
+            words = z_raw[c][:].bitcast(F32)
+            bank = psum.tile([P, S, P], F32, name="turned%d" % t, tag="bank%d" % (t % T_BANKS))
+            for s in range(S):
+                nc.tensor.transpose(bank[:, s, :], words[:, s, k * P:(k + 1) * P], ident[:])
+            turned[t] = bank
 
-        def transposes(q):
-            for i in range(4):
-                c, k = zsrc[4 * q + i]
-                zf = zch[c][:].bitcast(F32)
-                xt = psum.tile([P, S, P], F32, name="xt%d_%d" % (q, i), tag="bank%d" % i)
-                for s in range(S):
-                    nc.tensor.transpose(xt[:, s, :], zf[:, s, k * P:(k + 1) * P], ident[:])
-                xts[(q, i)] = xt
+        def evacuate(t):
+            gt = gpool.tile([P, 2, P, 4], BF16, name="grouped%d" % t, tag="grouped", align_bytes=64)
+            nc.scalar.copy(out=gt[:].bitcast(F32), in_=turned[t][:].rearrange("q (g u) r -> q g r u", u=2))
+            grouped[t] = gt
 
-        def evacuate(q):
-            for a in range(2):
-                gt = gpool.tile([P, 2, 2, P, 4], BF16, name="gt%d_%d" % (q, a), tag="gt", align_bytes=64)
-                for i2 in range(2):
-                    nc.scalar.copy(out=gt[:, i2].bitcast(F32),
-                                   in_=xts[(q, 2 * a + i2)][:].rearrange("q (g u) r -> q g r u", u=2))
-                grp[2 * q + a] = gt
+        def quantise(t):
+            nc.vector.quantize_mx(out=z_codes[t][:].bitcast(FP8X4), scales=z_scales[t][:],
+                                  in_=grouped[t][:].rearrange("q g r t -> q (g r t)"))
 
-        def quantise(j):
-            nc.vector.quantize_mx(out=z_codes[j][:].bitcast(FP8X4), scales=z_scales[j][:],
-                                  in_=grp[j][:].rearrange("q i g r t -> q (i g r t)"))
+        def multiply(t, bank):
+            j = t // 2
+            if t % 2 == 0:
+                y_ps[j] = psum.tile([P, 2 * V], F32, name="y_ps%d_%d" % (j, bank), tag="bank%d" % bank)
+                bank_of[j] = bank
+            c0 = (t % 2) * V
+            for g in range(2):
+                nc.tensor.matmul_mx(out=y_ps[j][:, c0:c0 + V],
+                                    lhsT=z_codes[t][:, g * P:(g + 1) * P].bitcast(FP8X4),
+                                    lhsT_scale=z_scales[t][:, g * P:(g + 1) * P],
+                                    rhs=a_codes[:, g * V:(g + 1) * V].bitcast(FP8X4),
+                                    rhs_scale=a_scales[:, g * V:(g + 1) * V],
+                                    start=(g == 0), stop=(g == 1))
 
-        def multiply(j, bank):
-            yb = psum.tile([P, 512], F32, name="yb%d_%d" % (j, bank), tag="bank%d" % bank)
-            for i2 in range(2):
-                for g in range(2):
-                    c0 = (2 * i2 + g) * P
-                    nc.tensor.matmul_mx(out=yb[:, i2 * V:(i2 + 1) * V],
-                                        lhsT=z_codes[j][:, c0:c0 + P].bitcast(FP8X4),
-                                        lhsT_scale=z_scales[j][:, c0:c0 + P],
-                                        rhs=a_codes[:, g * V:(g + 1) * V].bitcast(FP8X4),
-                                        rhs_scale=a_scales[:, g * V:(g + 1) * V],
-                                        start=(g == 0), stop=(g == 1))
-            ybank[j] = yb
-
-        def statistics(j):
-            if j < NE:
-                nc.vector.bn_stats(out=stats[:, j, :], in_=ybank[j][:])
-            else:
-                nc.vector.bn_stats(out=late[:, 3 + 6 * (j - NE):9 + 6 * (j - NE)], in_=ybank[j][:])
-
-        transposes(0)
-        evacuate(0)
-        quantise(0)
-        quantise(1)
-        for q in range(1, NQ + 1):
-            if q < NQ:
-                transposes(q)
-            for a in range(2):
-                multiply(2 * (q - 1) + a, 4 + 2 * ((q - 1) % 2) + a)
-            if q == 4:
-                spread_gb_tensor(4)
-            if q < NQ:
-                evacuate(q)
-                quantise(2 * q)
-            else:
-                early = const.tile([P, 2], F32, name="early")
-                nc.vector.bn_aggr(out=early[:], in_=stats[:].rearrange("p j k -> p (j k)"))
-                nc.vector.tensor_tensor(out=late[:, 1:3], in0=early[:], in1=weight[:], op=ALU.mult)
-            statistics(2 * (q - 1))
-            statistics(2 * (q - 1) + 1)
-            if q < NQ:
-                quantise(2 * q + 1)
-            if q == 3:
-                spread_gb_vector()
-            if q == 4:
-                spread_gb_out()
-
-        multiply(0, 0)
-        multiply(1, 1)
+        groups = [list(range(t0, min(t0 + GROUP, TILES))) for t0 in range(0, TILES, GROUP)]
+        n_groups = len(groups)
+        counted = 0
+        for i in range(n_groups + 1):
+            now = groups[i] if i < n_groups else []
+            before = groups[i - 1] if i > 0 else []
+            for t in now:
+                transposes(t)
+            for t in before:
+                multiply(t, T_BANKS + (t // 2) % Y_BANKS)
+            if i == n_groups // 2:
+                spread_matmul()
+            for t in now:
+                evacuate(t)
+            full = (before[-1] + 1) // 2 if before else 0
+            todo = list(now)
+            while todo or counted < full:
+                for t in todo[:2]:
+                    quantise(t)
+                todo = todo[2:]
+                if counted < full:
+                    nc.vector.bn_stats(out=stats[:, counted, :], in_=y_ps[counted][:])
+                    counted += 1
+            if i == n_groups // 2 - 1:
+                spread_rows()
+            if i == n_groups // 2:
+                spread_out()
 
         mom = const.tile([P, 2], F32, name="mom")
-        nc.vector.bn_aggr(out=mom[:], in_=late[:])
+        nc.vector.bn_aggr(out=mom[:], in_=stats[:].rearrange("p j k -> p (j k)"))
         nc.vector.scalar_tensor_tensor(out=mom[:, 1:2], in0=mom[:, 0:1], scalar=mom[:, 0:1], in1=mom[:, 1:2],
                                        op0=ALU.mult, op1=ALU.add)
-        mom_ps = psum.tile([P, 2], F32, name="mom_ps", tag="bank3")
-        nc.tensor.matmul(out=mom_ps[:], lhsT=pair[:].rearrange("p o r -> p (o r)"), rhs=mom[:], start=True, stop=True)
+        mom_ps = psum.tile([P, 2], F32, name="mom_ps", tag="bank%d" % MISC_BANK)
+        nc.tensor.matmul(out=mom_ps[:], lhsT=pair_avg[:].rearrange("p o r -> p (o r)"), rhs=mom[:],
+                         start=True, stop=True)
+
+        order = list(range(PAIRS - 4, PAIRS)) + list(range(PAIRS - 4))
+        again = [j for j in order if j < PAIRS - Y_BANKS]
+        free = list(range(T_BANKS))
+        done = [0]
+
+        def refill():
+            while free and done[0] < len(again):
+                j = again[done[0]]
+                bank = free[0]
+                free[:] = free[1:]
+                multiply(2 * j, bank)
+                multiply(2 * j + 1, bank)
+                done[0] += 1
+
+        refill()
+
         negvar = const.tile([P, 1], F32, name="negvar")
         nc.vector.tensor_scalar(out=negvar[:], in0=mom_ps[:, 0:1], scalar1=mom_ps[:, 0:1], scalar2=mom_ps[:, 1:2],
                                 op0=ALU.mult, op1=ALU.subtract)
@@ -205,31 +203,24 @@ def tile_dggcn_sparse_assemble_pa_kernel(tc, z, A, x, gamma, beta, out):
         nc.scalar.activation(out=std[:], in_=negvar[:], func=ACT.Sqrt, bias=eps_t[:, 0:1], scale=-1.0)
         rstd = const.tile([P, 1], F32, name="rstd")
         nc.vector.reciprocal(out=rstd[:], in_=std[:])
-        sc2 = const.tile([P, 2], F32, name="sc2")
-        nc.vector.tensor_scalar(out=sc2[:], in0=gn[:], scalar1=rstd[:, 0:1], scalar2=None, op0=ALU.mult)
+        scale_pm = const.tile([P, 2], F32, name="scale_pm")
+        nc.vector.tensor_scalar(out=scale_pm[:], in0=gamma_pm[:], scalar1=rstd[:, 0:1], scalar2=None, op0=ALU.mult)
         shift = const.tile([P, 1], F32, name="shift")
-        nc.vector.scalar_tensor_tensor(out=shift[:], in0=mom_ps[:, 0:1], scalar=sc2[:, 1:2], in1=beta_f[:],
+        nc.vector.scalar_tensor_tensor(out=shift[:], in0=mom_ps[:, 0:1], scalar=scale_pm[:, 1:2], in1=beta_f[:],
                                        op0=ALU.mult, op1=ALU.add)
 
-        multiply(2, 2)
-        multiply(3, 3)
-
-        order = [12, 13, 14, 15] + list(range(12))
-        banks = [4, 5, 6, 7, 0, 1, 2, 3]
         res = {}
-        for n in range(16):
-            j = order[n]
+        for j in order:
             b = j // 4
-            c0 = (j % 4) * 512
-            hq = j % 2
-            if hq == 0:
-                res[j // 2] = tpool.tile([P, 1024], F32, name="res%d" % (j // 2), tag="res")
-            rt = res[j // 2]
-            nc.vector.scalar_tensor_tensor(out=rt[:, hq * 512:(hq + 1) * 512], in0=ybank[j][:], scalar=sc2[:, 0:1],
-                                           in1=xs[b][:, c0:c0 + 512], op0=ALU.mult, op1=ALU.add)
-            if hq == 1:
-                nc.scalar.activation(out=rt[:], in_=rt[:], func=ACT.Relu, bias=shift[:, 0:1], scale=1.0)
-                q0 = ((j % 4) // 2) * 1024
-                nc.sync.dma_start(out=ov[b, :, q0:q0 + 1024], in_=rt[:])
-            if n + 8 < 16:
-                multiply(order[n + 8], banks[n % 8])
+            c0 = (j % 4) * 2 * V
+            h = j % 2
+            if h == 0:
+                res[j // 2] = rpool.tile([P, 4 * V], F32, name="res%d" % (j // 2), tag="res")
+            part = res[j // 2][:, h * 2 * V:(h + 1) * 2 * V]
+            nc.vector.scalar_tensor_tensor(out=part, in0=y_ps[j][:], scalar=scale_pm[:, 0:1],
+                                           in1=x_sb[b][:, c0:c0 + 2 * V], op0=ALU.mult, op1=ALU.add)
+            nc.scalar.activation(out=part, in_=part, func=ACT.Relu, bias=shift[:, 0:1], scale=1.0)
+            if h == 1:
+                nc.sync.dma_start(out=ov[b, :, c0 - 2 * V:c0 + 2 * V], in_=res[j // 2][:])
+            free.append(bank_of[j])
+            refill()

@@ -18,7 +18,7 @@ FLOPS = 2 * B * O * T * S * V * V
 
 TILES = B * O * T // P
 PAIRS = TILES // 2
-GROUP = 4
+GROUP = 3
 T_BANKS = GROUP
 Y_BANKS = 7 - GROUP
 MISC_BANK = 7

@@ -18,7 +18,7 @@ FLOPS = 2 * B * O * T * S * V * V
 
 TILES = B * O * T // P
 PAIRS = TILES // 2
-GROUP = 3
+GROUP = 4
 T_BANKS = GROUP
 Y_BANKS = 7 - GROUP
 MISC_BANK = 7
@@ -90,17 +90,20 @@ def tile_dggcn_sparse_assemble_pa_kernel(tc, z, A, x, gamma, beta, out):
         gb_wide = const.tile([P, O, 2], F32, name="gb_wide")
         gamma_pm = const.tile([P, 2], F32, name="gamma_pm")
         beta_f = const.tile([P, 1], F32, name="beta_f")
-        gb_ps = psum.tile([P, 2], F32, name="gb_ps", tag="bank%d" % MISC_BANK)
+        gb_box = {}
 
         def spread_rows():
             nc.vector.tensor_tensor(out=gb_wide[:], in0=gb_rows[:, 0:O].unsqueeze(2).to_broadcast([P, O, 2]),
                                     in1=gb_rows[:, O:2 * O].unsqueeze(2).to_broadcast([P, O, 2]), op=ALU.add)
 
         def spread_matmul():
+            gb_ps = psum.tile([P, 2], F32, name="gb_ps", tag="bank%d" % MISC_BANK)
+            gb_box[0] = gb_ps
             nc.tensor.matmul(out=gb_ps[:], lhsT=gb_wide[:].rearrange("p o r -> p (o r)"), rhs=ident[:, 0:2],
                              start=True, stop=True)
 
         def spread_out():
+            gb_ps = gb_box[0]
             nc.vector.tensor_copy(out=gamma_pm[:, 0:1], in_=gb_ps[:, 0:1])
             nc.vector.tensor_scalar(out=gamma_pm[:, 1:2], in0=gb_ps[:, 0:1], scalar1=-1.0, scalar2=None, op0=ALU.mult)
             nc.vector.tensor_copy(out=beta_f[:], in_=gb_ps[:, 1:2])
@@ -113,8 +116,13 @@ def tile_dggcn_sparse_assemble_pa_kernel(tc, z, A, x, gamma, beta, out):
         y_ps = {}
         bank_of = {}
 
+        idle_ps = psum.tile([P, P], F32, name="idle_ps", tag="bank%d" % MISC_BANK)
+
         def transposes(t):
             c, k = where[t]
+            if k == 0 and c < 3:
+                for n in range(3):
+                    nc.tensor.matmul(out=idle_ps[:], lhsT=ident[:], rhs=ident[:], start=True, stop=True)
             words = z_raw[c][:].bitcast(F32)
             bank = psum.tile([P, S, P], F32, name="turned%d" % t, tag="bank%d" % (t % T_BANKS))
             for s in range(S):

@@ -17,22 +17,26 @@ EPS = 1e-5
 FLOPS = 2 * B * O * T * S * V * V
 
 TILES = B * O * T // P
+TILES_PER_B = TILES // B
 PAIRS = TILES // 2
+PAIRS_PER_B = PAIRS // B
+PASSES = 2
+PACK = 4
+BN_STATS = 6
+
 GROUP = 4
 T_BANKS = GROUP
 Y_BANKS = 7 - GROUP
-MISC_BANK = 7
-PIN = True
+SMALL_BANK = 7
 
 
 def tile_dggcn_sparse_assemble_pa_kernel(tc, z, A, x, gamma, beta, out):
     nc = tc.nc
     with ExitStack() as ctx:
-        if PIN:
-            ctx.enter_context(tc.manual_schedule())
+        ctx.enter_context(tc.manual_schedule())
         const = ctx.enter_context(tc.tile_pool(name="const", bufs=1))
         keep = ctx.enter_context(tc.tile_pool(name="keep", bufs=1))
-        gpool = ctx.enter_context(tc.tile_pool(name="gpool", bufs=8))
+        gpool = ctx.enter_context(tc.tile_pool(name="gpool", bufs=2 * GROUP))
         rpool = ctx.enter_context(tc.tile_pool(name="rpool", bufs=4))
         psum = ctx.enter_context(tc.psum_pool(name="psum", bufs=1))
 
@@ -43,25 +47,25 @@ def tile_dggcn_sparse_assemble_pa_kernel(tc, z, A, x, gamma, beta, out):
 
         gb_rows = const.tile([P, 2 * O], BF16, name="gb_rows")
         nc.vector.memset(gb_rows[:], 0.0)
-        nc.scalar.dma_start(out=gb_rows[0:1, 0:O], in_=gamma.rearrange("(u o) -> u o", u=1))
-        nc.scalar.dma_start(out=gb_rows[1:2, O:2 * O], in_=beta.rearrange("(u o) -> u o", u=1))
+        nc.scalar.dma_start(out=gb_rows[0:1, 0:O], in_=gamma.rearrange("(a o) -> a o", a=1))
+        nc.scalar.dma_start(out=gb_rows[1:2, O:2 * O], in_=beta.rearrange("(a o) -> a o", a=1))
 
-        chunks = [2, 2] + [4] * (TILES // 4 - 1)
-        z_raw = [keep.tile([P, S, n * V], BF16, name="z_raw%d" % c) for c, n in enumerate(chunks)]
-        where = [(c, k) for c, n in enumerate(chunks) for k in range(n)]
+        chunks = [2] * 6 + [4] * (TILES // 4 - 3)
+        z_raw = [keep.tile([P, S, size * V], BF16, name="z_raw%d" % c) for c, size in enumerate(chunks)]
+        where = [(c, at) for c, size in enumerate(chunks) for at in range(size)]
         a_raw = const.tile([P, 2 * S, V], BF16, name="a_raw")
-        x_sb = [keep.tile([P, 8 * V], BF16, name="x_sb%d" % b) for b in range(B)]
+        x_sb = [keep.tile([P, TILES_PER_B * V], BF16, name="x_sb%d" % b) for b in range(B)]
 
         def load_z(c):
-            t0 = sum(chunks[:c])
-            c0 = (t0 % 8) * V
-            nc.sync.dma_start(out=z_raw[c][:], in_=zv[t0 // 8, :, :, c0:c0 + chunks[c] * V])
+            first = sum(chunks[:c])
+            col = (first % TILES_PER_B) * V
+            nc.sync.dma_start(out=z_raw[c][:], in_=zv[first // TILES_PER_B, :, :, col:col + chunks[c] * V])
 
         load_z(0)
         nc.sync.dma_start(out=a_raw[:].rearrange("q (s e) w -> q s (e w)", e=2), in_=av)
         for c in range(1, len(chunks)):
             load_z(c)
-        for b in (3, 0, 1, 2):
+        for b in [B - 1] + list(range(B - 1)):
             nc.sync.dma_start(out=x_sb[b][:], in_=xv[b])
 
         ident = const.tile([P, P], F32, name="ident")
@@ -72,137 +76,129 @@ def tile_dggcn_sparse_assemble_pa_kernel(tc, z, A, x, gamma, beta, out):
         nc.scalar.activation(out=warm[:], in_=one[:], func=ACT.Sqrt)
         eps_t = const.tile([P, 1], F32, name="eps_t")
         nc.vector.memset(eps_t[:], EPS)
-        idv = ident[:].rearrange("p (o r) -> p o r", r=2)
+        id_pairs = ident[:].rearrange("p (o d) -> p o d", d=2)
         half = const.tile([P, O], F32, name="half")
-        nc.vector.tensor_tensor(out=half[:], in0=idv[:, :, 0], in1=idv[:, :, 1], op=ALU.add)
+        nc.vector.tensor_tensor(out=half[:], in0=id_pairs[:, :, 0], in1=id_pairs[:, :, 1], op=ALU.add)
         pair_avg = const.tile([P, O, 2], F32, name="pair_avg")
         nc.vector.tensor_scalar(out=pair_avg[:], in0=half[:].unsqueeze(2).to_broadcast([P, O, 2]),
                                 scalar1=0.5, scalar2=None, op0=ALU.mult)
 
-        a_grp = const.tile([P, 2, V, 4], BF16, name="a_grp", align_bytes=64)
-        for g in range(2):
-            nc.vector.tensor_copy(out=a_grp[:, g], in_=a_raw[:, 4 * g:4 * g + 4, :].rearrange("q t w -> q w t"))
-        a_codes = const.tile([P, 2 * V], U32, name="a_codes", align_bytes=64)
-        a_scales = const.tile([P, 2 * V], U8, name="a_scales", align_bytes=64)
+        a_grp = const.tile([P, PASSES, V, PACK], BF16, name="a_grp", align_bytes=64)
+        for g in range(PASSES):
+            nc.vector.tensor_copy(out=a_grp[:, g],
+                                  in_=a_raw[:, PACK * g:PACK * (g + 1), :].rearrange("q j w -> q w j"))
+        a_codes = const.tile([P, PASSES * V], U32, name="a_codes", align_bytes=64)
+        a_scales = const.tile([P, PASSES * V], U8, name="a_scales", align_bytes=64)
         nc.vector.quantize_mx(out=a_codes[:].bitcast(FP8X4), scales=a_scales[:],
-                              in_=a_grp[:].rearrange("q g w t -> q (g w t)"))
+                              in_=a_grp[:].rearrange("q g w j -> q (g w j)"))
 
         gb_wide = const.tile([P, O, 2], F32, name="gb_wide")
         gamma_pm = const.tile([P, 2], F32, name="gamma_pm")
         beta_f = const.tile([P, 1], F32, name="beta_f")
-        gb_box = {}
+        gb_ps = psum.tile([P, 2], F32, name="gb_ps", tag="bank%d" % SMALL_BANK)
 
-        def spread_rows():
+        def gamma_beta_twice():
             nc.vector.tensor_tensor(out=gb_wide[:], in0=gb_rows[:, 0:O].unsqueeze(2).to_broadcast([P, O, 2]),
                                     in1=gb_rows[:, O:2 * O].unsqueeze(2).to_broadcast([P, O, 2]), op=ALU.add)
 
-        def spread_matmul():
-            gb_ps = psum.tile([P, 2], F32, name="gb_ps", tag="bank%d" % MISC_BANK)
-            gb_box[0] = gb_ps
-            nc.tensor.matmul(out=gb_ps[:], lhsT=gb_wide[:].rearrange("p o r -> p (o r)"), rhs=ident[:, 0:2],
+        def gamma_beta_to_partitions():
+            nc.tensor.matmul(out=gb_ps[:], lhsT=gb_wide[:].rearrange("p o d -> p (o d)"), rhs=ident[:, 0:2],
                              start=True, stop=True)
 
-        def spread_out():
-            gb_ps = gb_box[0]
+        def gamma_beta_out():
             nc.vector.tensor_copy(out=gamma_pm[:, 0:1], in_=gb_ps[:, 0:1])
             nc.vector.tensor_scalar(out=gamma_pm[:, 1:2], in0=gb_ps[:, 0:1], scalar1=-1.0, scalar2=None, op0=ALU.mult)
             nc.vector.tensor_copy(out=beta_f[:], in_=gb_ps[:, 1:2])
 
-        z_codes = [keep.tile([P, 2 * P], U32, name="z_codes%d" % t, align_bytes=64) for t in range(TILES)]
-        z_scales = [keep.tile([P, 2 * P], U8, name="z_scales%d" % t, align_bytes=64) for t in range(TILES)]
-        stats = const.tile([P, PAIRS, 6], F32, name="stats")
+        z_codes = [keep.tile([P, PASSES * P], U32, name="z_codes%d" % i, align_bytes=64) for i in range(TILES)]
+        z_scales = [keep.tile([P, PASSES * P], U8, name="z_scales%d" % i, align_bytes=64) for i in range(TILES)]
+        stats = const.tile([P, PAIRS, BN_STATS], F32, name="stats")
         turned = {}
         grouped = {}
         y_ps = {}
         bank_of = {}
 
-        idle_ps = psum.tile([P, P], F32, name="idle_ps", tag="bank%d" % MISC_BANK)
-
-        def transposes(t):
-            c, k = where[t]
-            if k == 0 and c < 3:
-                for n in range(3):
-                    nc.tensor.matmul(out=idle_ps[:], lhsT=ident[:], rhs=ident[:], start=True, stop=True)
+        def transposes(i):
+            c, at = where[i]
             words = z_raw[c][:].bitcast(F32)
-            bank = psum.tile([P, S, P], F32, name="turned%d" % t, tag="bank%d" % (t % T_BANKS))
+            turned[i] = psum.tile([P, S, P], F32, name="turned%d" % i, tag="bank%d" % (i % T_BANKS))
             for s in range(S):
-                nc.tensor.transpose(bank[:, s, :], words[:, s, k * P:(k + 1) * P], ident[:])
-            turned[t] = bank
+                nc.tensor.transpose(turned[i][:, s, :], words[:, s, at * P:(at + 1) * P], ident[:])
 
-        def evacuate(t):
-            gt = gpool.tile([P, 2, P, 4], BF16, name="grouped%d" % t, tag="grouped", align_bytes=64)
-            nc.scalar.copy(out=gt[:].bitcast(F32), in_=turned[t][:].rearrange("q (g u) r -> q g r u", u=2))
-            grouped[t] = gt
+        def copy_out(i):
+            grouped[i] = gpool.tile([P, PASSES, P, PACK], BF16, name="grouped%d" % i, tag="grouped", align_bytes=64)
+            nc.scalar.copy(out=grouped[i][:].bitcast(F32), in_=turned[i][:].rearrange("q (g u) r -> q g r u", u=2))
 
-        def quantise(t):
-            nc.vector.quantize_mx(out=z_codes[t][:].bitcast(FP8X4), scales=z_scales[t][:],
-                                  in_=grouped[t][:].rearrange("q g r t -> q (g r t)"))
+        def quantise(i):
+            nc.vector.quantize_mx(out=z_codes[i][:].bitcast(FP8X4), scales=z_scales[i][:],
+                                  in_=grouped[i][:].rearrange("q g r j -> q (g r j)"))
 
-        def multiply(t, bank):
-            j = t // 2
-            if t % 2 == 0:
-                y_ps[j] = psum.tile([P, 2 * V], F32, name="y_ps%d_%d" % (j, bank), tag="bank%d" % bank)
-                bank_of[j] = bank
-            c0 = (t % 2) * V
-            for g in range(2):
-                nc.tensor.matmul_mx(out=y_ps[j][:, c0:c0 + V],
-                                    lhsT=z_codes[t][:, g * P:(g + 1) * P].bitcast(FP8X4),
-                                    lhsT_scale=z_scales[t][:, g * P:(g + 1) * P],
+        def multiply(i, bank):
+            n = i // 2
+            if i % 2 == 0:
+                y_ps[n] = psum.tile([P, 2 * V], F32, name="y_ps%d_%d" % (n, bank), tag="bank%d" % bank)
+                bank_of[n] = bank
+            col = (i % 2) * V
+            for g in range(PASSES):
+                nc.tensor.matmul_mx(out=y_ps[n][:, col:col + V],
+                                    lhsT=z_codes[i][:, g * P:(g + 1) * P].bitcast(FP8X4),
+                                    lhsT_scale=z_scales[i][:, g * P:(g + 1) * P],
                                     rhs=a_codes[:, g * V:(g + 1) * V].bitcast(FP8X4),
                                     rhs_scale=a_scales[:, g * V:(g + 1) * V],
-                                    start=(g == 0), stop=(g == 1))
+                                    start=(g == 0), stop=(g == PASSES - 1))
 
-        groups = [list(range(t0, min(t0 + GROUP, TILES))) for t0 in range(0, TILES, GROUP)]
-        n_groups = len(groups)
+        groups = [list(range(first, first + GROUP)) for first in range(0, TILES, GROUP)]
+        rounds = len(groups)
         counted = 0
-        for i in range(n_groups + 1):
-            now = groups[i] if i < n_groups else []
-            before = groups[i - 1] if i > 0 else []
-            for t in now:
-                transposes(t)
-            for t in before:
-                multiply(t, T_BANKS + (t // 2) % Y_BANKS)
-            if i == n_groups // 2:
-                spread_matmul()
-            for t in now:
-                evacuate(t)
+        for m in range(rounds + 1):
+            now = groups[m] if m < rounds else []
+            before = groups[m - 1] if m > 0 else []
+            for i in now:
+                transposes(i)
+            for i in before:
+                multiply(i, T_BANKS + (i // 2) % Y_BANKS)
+            if m == rounds // 2:
+                gamma_beta_to_partitions()
+            for i in now:
+                copy_out(i)
             full = (before[-1] + 1) // 2 if before else 0
             todo = list(now)
             while todo or counted < full:
-                for t in todo[:2]:
-                    quantise(t)
+                for i in todo[:2]:
+                    quantise(i)
                 todo = todo[2:]
                 if counted < full:
                     nc.vector.bn_stats(out=stats[:, counted, :], in_=y_ps[counted][:])
                     counted += 1
-            if i == n_groups // 2 - 1:
-                spread_rows()
-            if i == n_groups // 2:
-                spread_out()
+            if m == rounds // 2 - 1:
+                gamma_beta_twice()
+            if m == rounds // 2:
+                gamma_beta_out()
+
+        last_b = PAIRS - PAIRS_PER_B
+        order = [last_b + 2, last_b + 3, last_b, last_b + 1] + list(range(last_b))
+        again = [n for n in order if n < PAIRS - Y_BANKS]
+        free = list(range(T_BANKS))
+
+        def multiply_again(most):
+            count = min(len(free), len(again), most)
+            for n, bank in zip(again[:count], free[:count]):
+                multiply(2 * n, bank)
+                multiply(2 * n + 1, bank)
+            again[:] = again[count:]
+            free[:] = free[count:]
+
+        multiply_again(2)
 
         mom = const.tile([P, 2], F32, name="mom")
-        nc.vector.bn_aggr(out=mom[:], in_=stats[:].rearrange("p j k -> p (j k)"))
+        nc.vector.bn_aggr(out=mom[:], in_=stats[:].rearrange("p n f -> p (n f)"))
         nc.vector.scalar_tensor_tensor(out=mom[:, 1:2], in0=mom[:, 0:1], scalar=mom[:, 0:1], in1=mom[:, 1:2],
                                        op0=ALU.mult, op1=ALU.add)
-        mom_ps = psum.tile([P, 2], F32, name="mom_ps", tag="bank%d" % MISC_BANK)
-        nc.tensor.matmul(out=mom_ps[:], lhsT=pair_avg[:].rearrange("p o r -> p (o r)"), rhs=mom[:],
+        mom_ps = psum.tile([P, 2], F32, name="mom_ps", tag="bank%d" % SMALL_BANK)
+        nc.tensor.matmul(out=mom_ps[:], lhsT=pair_avg[:].rearrange("p o d -> p (o d)"), rhs=mom[:],
                          start=True, stop=True)
 
-        order = list(range(PAIRS - 4, PAIRS)) + list(range(PAIRS - 4))
-        again = [j for j in order if j < PAIRS - Y_BANKS]
-        free = list(range(T_BANKS))
-        done = [0]
-
-        def refill():
-            while free and done[0] < len(again):
-                j = again[done[0]]
-                bank = free[0]
-                free[:] = free[1:]
-                multiply(2 * j, bank)
-                multiply(2 * j + 1, bank)
-                done[0] += 1
-
-        refill()
+        multiply_again(T_BANKS)
 
         negvar = const.tile([P, 1], F32, name="negvar")
         nc.vector.tensor_scalar(out=negvar[:], in0=mom_ps[:, 0:1], scalar1=mom_ps[:, 0:1], scalar2=mom_ps[:, 1:2],
@@ -218,17 +214,17 @@ def tile_dggcn_sparse_assemble_pa_kernel(tc, z, A, x, gamma, beta, out):
                                        op0=ALU.mult, op1=ALU.add)
 
         res = {}
-        for j in order:
-            b = j // 4
-            c0 = (j % 4) * 2 * V
-            h = j % 2
-            if h == 0:
-                res[j // 2] = rpool.tile([P, 4 * V], F32, name="res%d" % (j // 2), tag="res")
-            part = res[j // 2][:, h * 2 * V:(h + 1) * 2 * V]
-            nc.vector.scalar_tensor_tensor(out=part, in0=y_ps[j][:], scalar=scale_pm[:, 0:1],
-                                           in1=x_sb[b][:, c0:c0 + 2 * V], op0=ALU.mult, op1=ALU.add)
+        for n in order:
+            b = n // PAIRS_PER_B
+            col = (n % PAIRS_PER_B) * 2 * V
+            second = n % 2
+            if not second:
+                res[n // 2] = rpool.tile([P, 4 * V], F32, name="res%d" % (n // 2), tag="res")
+            part = res[n // 2][:, second * 2 * V:(second + 1) * 2 * V]
+            nc.vector.scalar_tensor_tensor(out=part, in0=y_ps[n][:], scalar=scale_pm[:, 0:1],
+                                           in1=x_sb[b][:, col:col + 2 * V], op0=ALU.mult, op1=ALU.add)
             nc.scalar.activation(out=part, in_=part, func=ACT.Relu, bias=shift[:, 0:1], scale=1.0)
-            if h == 1:
-                nc.sync.dma_start(out=ov[b, :, c0 - 2 * V:c0 + 2 * V], in_=res[j // 2][:])
-            free.append(bank_of[j])
-            refill()
+            if second:
+                nc.sync.dma_start(out=ov[b, :, col - 2 * V:col + 2 * V], in_=res[n // 2][:])
+            free.append(bank_of[n])
+            multiply_again(1)

@@ -20,6 +20,7 @@ TILES = B * O * T // P
 TILES_PER_B = TILES // B
 PAIRS = TILES // 2
 PAIRS_PER_B = PAIRS // B
+CHUNK = 4
 PASSES = 2
 PACK = 4
 BN_STATS = 6
@@ -50,20 +51,18 @@ def tile_dggcn_sparse_assemble_pa_kernel(tc, z, A, x, gamma, beta, out):
         nc.scalar.dma_start(out=gb_rows[0:1, 0:O], in_=gamma.rearrange("(a o) -> a o", a=1))
         nc.scalar.dma_start(out=gb_rows[1:2, O:2 * O], in_=beta.rearrange("(a o) -> a o", a=1))
 
-        chunks = [2] * 6 + [4] * (TILES // 4 - 3)
-        z_raw = [keep.tile([P, S, size * V], BF16, name="z_raw%d" % c) for c, size in enumerate(chunks)]
-        where = [(c, at) for c, size in enumerate(chunks) for at in range(size)]
+        z_raw = [keep.tile([P, S, CHUNK * V], BF16, name="z_raw%d" % c) for c in range(TILES // CHUNK)]
         a_raw = const.tile([P, 2 * S, V], BF16, name="a_raw")
         x_sb = [keep.tile([P, TILES_PER_B * V], BF16, name="x_sb%d" % b) for b in range(B)]
 
         def load_z(c):
-            first = sum(chunks[:c])
+            first = c * CHUNK
             col = (first % TILES_PER_B) * V
-            nc.sync.dma_start(out=z_raw[c][:], in_=zv[first // TILES_PER_B, :, :, col:col + chunks[c] * V])
+            nc.sync.dma_start(out=z_raw[c][:], in_=zv[first // TILES_PER_B, :, :, col:col + CHUNK * V])
 
         load_z(0)
         nc.sync.dma_start(out=a_raw[:].rearrange("q (s e) w -> q s (e w)", e=2), in_=av)
-        for c in range(1, len(chunks)):
+        for c in range(1, TILES // CHUNK):
             load_z(c)
         for b in [B - 1] + list(range(B - 1)):
             nc.sync.dma_start(out=x_sb[b][:], in_=xv[b])
@@ -119,8 +118,8 @@ def tile_dggcn_sparse_assemble_pa_kernel(tc, z, A, x, gamma, beta, out):
         bank_of = {}
 
         def transposes(i):
-            c, at = where[i]
-            words = z_raw[c][:].bitcast(F32)
+            at = i % CHUNK
+            words = z_raw[i // CHUNK][:].bitcast(F32)
             turned[i] = psum.tile([P, S, P], F32, name="turned%d" % i, tag="bank%d" % (i % T_BANKS))
             for s in range(S):
                 nc.tensor.transpose(turned[i][:, s, :], words[:, s, at * P:(at + 1) * P], ident[:])
@@ -175,21 +174,6 @@ def tile_dggcn_sparse_assemble_pa_kernel(tc, z, A, x, gamma, beta, out):
             if m == rounds // 2:
                 gamma_beta_out()
 
-        last_b = PAIRS - PAIRS_PER_B
-        order = [last_b + 2, last_b + 3, last_b, last_b + 1] + list(range(last_b))
-        again = [n for n in order if n < PAIRS - Y_BANKS]
-        free = list(range(T_BANKS))
-
-        def multiply_again(most):
-            count = min(len(free), len(again), most)
-            for n, bank in zip(again[:count], free[:count]):
-                multiply(2 * n, bank)
-                multiply(2 * n + 1, bank)
-            again[:] = again[count:]
-            free[:] = free[count:]
-
-        multiply_again(2)
-
         mom = const.tile([P, 2], F32, name="mom")
         nc.vector.bn_aggr(out=mom[:], in_=stats[:].rearrange("p n f -> p (n f)"))
         nc.vector.scalar_tensor_tensor(out=mom[:, 1:2], in0=mom[:, 0:1], scalar=mom[:, 0:1], in1=mom[:, 1:2],
@@ -198,7 +182,19 @@ def tile_dggcn_sparse_assemble_pa_kernel(tc, z, A, x, gamma, beta, out):
         nc.tensor.matmul(out=mom_ps[:], lhsT=pair_avg[:].rearrange("p o d -> p (o d)"), rhs=mom[:],
                          start=True, stop=True)
 
-        multiply_again(T_BANKS)
+        order = list(range(PAIRS - PAIRS_PER_B, PAIRS)) + list(range(PAIRS - PAIRS_PER_B))
+        again = [n for n in order if n < PAIRS - Y_BANKS]
+        free = list(range(T_BANKS))
+
+        def multiply_again():
+            count = min(len(free), len(again))
+            for n, bank in zip(again[:count], free[:count]):
+                multiply(2 * n, bank)
+                multiply(2 * n + 1, bank)
+            again[:] = again[count:]
+            free[:] = free[count:]
+
+        multiply_again()
 
         negvar = const.tile([P, 1], F32, name="negvar")
         nc.vector.tensor_scalar(out=negvar[:], in0=mom_ps[:, 0:1], scalar1=mom_ps[:, 0:1], scalar2=mom_ps[:, 1:2],
@@ -227,4 +223,4 @@ def tile_dggcn_sparse_assemble_pa_kernel(tc, z, A, x, gamma, beta, out):
             if second:
                 nc.sync.dma_start(out=ov[b, :, col - 2 * V:col + 2 * V], in_=res[n // 2][:])
             free.append(bank_of[n])
-            multiply_again(1)
+            multiply_again()

from contextlib import ExitStack

import concourse.mybir as mybir
from concourse.masks import make_identity

FP8X4 = mybir.dt.float8_e4m3fn_x4
BF16 = mybir.dt.bfloat16
F32 = mybir.dt.float32
U32 = mybir.dt.uint32
U8 = mybir.dt.uint8
ALU = mybir.AluOpType
ACT = mybir.ActivationFunctionType

S, B, O, T, V = 4, 4, 64, 16, 256
P = 128
EPS = 1e-5
FLOPS = 2 * B * O * T * S * V * V

TILES = B * O * T // P
TILES_PER_B = TILES // B
PAIRS = TILES // 2
PAIRS_PER_B = PAIRS // B
CHUNK = 4
PASSES = 2
PACK = 4
BN_STATS = 6

GROUP = 4
T_BANKS = GROUP
Y_BANKS = 7 - GROUP
SMALL_BANK = 7


def tile_dggcn_sparse_assemble_pa_kernel(tc, z, A, x, gamma, beta, out):
    nc = tc.nc
    with ExitStack() as ctx:
        ctx.enter_context(tc.manual_schedule())
        const = ctx.enter_context(tc.tile_pool(name="const", bufs=1))
        keep = ctx.enter_context(tc.tile_pool(name="keep", bufs=1))
        gpool = ctx.enter_context(tc.tile_pool(name="gpool", bufs=2 * GROUP))
        rpool = ctx.enter_context(tc.tile_pool(name="rpool", bufs=4))
        psum = ctx.enter_context(tc.psum_pool(name="psum", bufs=1))

        zv = z.rearrange("s b o (th tl) v -> b (o th) s (tl v)", th=2)
        xv = x.rearrange("b c (th tl) v -> b (c th) (tl v)", th=2)
        ov = out.rearrange("b c (th tl) v -> b (c th) (tl v)", th=2)
        av = A.rearrange("s (q e) w -> q s (e w)", e=2)

        gb_rows = const.tile([P, 2 * O], BF16, name="gb_rows")
        nc.vector.memset(gb_rows[:], 0.0)
        nc.scalar.dma_start(out=gb_rows[0:1, 0:O], in_=gamma.rearrange("(a o) -> a o", a=1))
        nc.scalar.dma_start(out=gb_rows[1:2, O:2 * O], in_=beta.rearrange("(a o) -> a o", a=1))

        z_raw = [keep.tile([P, S, CHUNK * V], BF16, name="z_raw%d" % c) for c in range(TILES // CHUNK)]
        a_raw = const.tile([P, 2 * S, V], BF16, name="a_raw")
        x_sb = [keep.tile([P, TILES_PER_B * V], BF16, name="x_sb%d" % b) for b in range(B)]

        def load_z(c):
            first = c * CHUNK
            col = (first % TILES_PER_B) * V
            nc.sync.dma_start(out=z_raw[c][:], in_=zv[first // TILES_PER_B, :, :, col:col + CHUNK * V])

        load_z(0)
        nc.sync.dma_start(out=a_raw[:].rearrange("q (s e) w -> q s (e w)", e=2), in_=av)
        for c in range(1, TILES // CHUNK):
            load_z(c)
        for b in [B - 1] + list(range(B - 1)):
            nc.sync.dma_start(out=x_sb[b][:], in_=xv[b])

        ident = const.tile([P, P], F32, name="ident")
        make_identity(nc, ident[:])
        one = const.tile([P, 1], F32, name="one")
        nc.vector.memset(one[:], 1.0)
        warm = const.tile([P, 1], F32, name="warm")
        nc.scalar.activation(out=warm[:], in_=one[:], func=ACT.Sqrt)
        eps_t = const.tile([P, 1], F32, name="eps_t")
        nc.vector.memset(eps_t[:], EPS)
        id_pairs = ident[:].rearrange("p (o d) -> p o d", d=2)
        half = const.tile([P, O], F32, name="half")
        nc.vector.tensor_tensor(out=half[:], in0=id_pairs[:, :, 0], in1=id_pairs[:, :, 1], op=ALU.add)
        pair_avg = const.tile([P, O, 2], F32, name="pair_avg")
        nc.vector.tensor_scalar(out=pair_avg[:], in0=half[:].unsqueeze(2).to_broadcast([P, O, 2]),
                                scalar1=0.5, scalar2=None, op0=ALU.mult)

        a_grp = const.tile([P, PASSES, V, PACK], BF16, name="a_grp", align_bytes=64)
        for g in range(PASSES):
            nc.vector.tensor_copy(out=a_grp[:, g],
                                  in_=a_raw[:, PACK * g:PACK * (g + 1), :].rearrange("q j w -> q w j"))
        a_codes = const.tile([P, PASSES * V], U32, name="a_codes", align_bytes=64)
        a_scales = const.tile([P, PASSES * V], U8, name="a_scales", align_bytes=64)
        nc.vector.quantize_mx(out=a_codes[:].bitcast(FP8X4), scales=a_scales[:],
                              in_=a_grp[:].rearrange("q g w j -> q (g w j)"))

        gb_wide = const.tile([P, O, 2], F32, name="gb_wide")
        gamma_pm = const.tile([P, 2], F32, name="gamma_pm")
        beta_f = const.tile([P, 1], F32, name="beta_f")
        gb_ps = psum.tile([P, 2], F32, name="gb_ps", tag="bank%d" % SMALL_BANK)

        def gamma_beta_twice():
            nc.vector.tensor_tensor(out=gb_wide[:], in0=gb_rows[:, 0:O].unsqueeze(2).to_broadcast([P, O, 2]),
                                    in1=gb_rows[:, O:2 * O].unsqueeze(2).to_broadcast([P, O, 2]), op=ALU.add)

        def gamma_beta_to_partitions():
            nc.tensor.matmul(out=gb_ps[:], lhsT=gb_wide[:].rearrange("p o d -> p (o d)"), rhs=ident[:, 0:2],
                             start=True, stop=True)

        def gamma_beta_out():
            nc.vector.tensor_copy(out=gamma_pm[:, 0:1], in_=gb_ps[:, 0:1])
            nc.vector.tensor_scalar(out=gamma_pm[:, 1:2], in0=gb_ps[:, 0:1], scalar1=-1.0, scalar2=None, op0=ALU.mult)
            nc.vector.tensor_copy(out=beta_f[:], in_=gb_ps[:, 1:2])

        z_codes = [keep.tile([P, PASSES * P], U32, name="z_codes%d" % i, align_bytes=64) for i in range(TILES)]
        z_scales = [keep.tile([P, PASSES * P], U8, name="z_scales%d" % i, align_bytes=64) for i in range(TILES)]
        stats = const.tile([P, PAIRS, BN_STATS], F32, name="stats")
        turned = {}
        grouped = {}
        y_ps = {}
        bank_of = {}

        def transposes(i):
            at = i % CHUNK
            words = z_raw[i // CHUNK][:].bitcast(F32)
            turned[i] = psum.tile([P, S, P], F32, name="turned%d" % i, tag="bank%d" % (i % T_BANKS))
            for s in range(S):
                nc.tensor.transpose(turned[i][:, s, :], words[:, s, at * P:(at + 1) * P], ident[:])

        def copy_out(i):
            grouped[i] = gpool.tile([P, PASSES, P, PACK], BF16, name="grouped%d" % i, tag="grouped", align_bytes=64)
            nc.scalar.copy(out=grouped[i][:].bitcast(F32), in_=turned[i][:].rearrange("q (g u) r -> q g r u", u=2))

        def quantise(i):
            nc.vector.quantize_mx(out=z_codes[i][:].bitcast(FP8X4), scales=z_scales[i][:],
                                  in_=grouped[i][:].rearrange("q g r j -> q (g r j)"))

        def multiply(i, bank):
            n = i // 2
            if i % 2 == 0:
                y_ps[n] = psum.tile([P, 2 * V], F32, name="y_ps%d_%d" % (n, bank), tag="bank%d" % bank)
                bank_of[n] = bank
            col = (i % 2) * V
            for g in range(PASSES):
                nc.tensor.matmul_mx(out=y_ps[n][:, col:col + V],
                                    lhsT=z_codes[i][:, g * P:(g + 1) * P].bitcast(FP8X4),
                                    lhsT_scale=z_scales[i][:, g * P:(g + 1) * P],
                                    rhs=a_codes[:, g * V:(g + 1) * V].bitcast(FP8X4),
                                    rhs_scale=a_scales[:, g * V:(g + 1) * V],
                                    start=(g == 0), stop=(g == PASSES - 1))

        groups = [list(range(first, first + GROUP)) for first in range(0, TILES, GROUP)]
        rounds = len(groups)
        counted = 0
        for m in range(rounds + 1):
            now = groups[m] if m < rounds else []
            before = groups[m - 1] if m > 0 else []
            for i in now:
                transposes(i)
            for i in before:
                multiply(i, T_BANKS + (i // 2) % Y_BANKS)
            if m == rounds // 2:
                gamma_beta_to_partitions()
            for i in now:
                copy_out(i)
            full = (before[-1] + 1) // 2 if before else 0
            todo = list(now)
            while todo or counted < full:
                for i in todo[:2]:
                    quantise(i)
                todo = todo[2:]
                if counted < full:
                    nc.vector.bn_stats(out=stats[:, counted, :], in_=y_ps[counted][:])
                    counted += 1
            if m == rounds // 2 - 1:
                gamma_beta_twice()
            if m == rounds // 2:
                gamma_beta_out()

        mom = const.tile([P, 2], F32, name="mom")
        nc.vector.bn_aggr(out=mom[:], in_=stats[:].rearrange("p n f -> p (n f)"))
        nc.vector.scalar_tensor_tensor(out=mom[:, 1:2], in0=mom[:, 0:1], scalar=mom[:, 0:1], in1=mom[:, 1:2],
                                       op0=ALU.mult, op1=ALU.add)
        mom_ps = psum.tile([P, 2], F32, name="mom_ps", tag="bank%d" % SMALL_BANK)
        nc.tensor.matmul(out=mom_ps[:], lhsT=pair_avg[:].rearrange("p o d -> p (o d)"), rhs=mom[:],
                         start=True, stop=True)

        order = list(range(PAIRS - PAIRS_PER_B, PAIRS)) + list(range(PAIRS - PAIRS_PER_B))
        again = [n for n in order if n < PAIRS - Y_BANKS]
        free = list(range(T_BANKS))

        def multiply_again():
            count = min(len(free), len(again))
            for n, bank in zip(again[:count], free[:count]):
                multiply(2 * n, bank)
                multiply(2 * n + 1, bank)
            again[:] = again[count:]
            free[:] = free[count:]

        multiply_again()

        negvar = const.tile([P, 1], F32, name="negvar")
        nc.vector.tensor_scalar(out=negvar[:], in0=mom_ps[:, 0:1], scalar1=mom_ps[:, 0:1], scalar2=mom_ps[:, 1:2],
                                op0=ALU.mult, op1=ALU.subtract)
        std = const.tile([P, 1], F32, name="std")
        nc.scalar.activation(out=std[:], in_=negvar[:], func=ACT.Sqrt, bias=eps_t[:, 0:1], scale=-1.0)
        rstd = const.tile([P, 1], F32, name="rstd")
        nc.vector.reciprocal(out=rstd[:], in_=std[:])
        scale_pm = const.tile([P, 2], F32, name="scale_pm")
        nc.vector.tensor_scalar(out=scale_pm[:], in0=gamma_pm[:], scalar1=rstd[:, 0:1], scalar2=None, op0=ALU.mult)
        shift = const.tile([P, 1], F32, name="shift")
        nc.vector.scalar_tensor_tensor(out=shift[:], in0=mom_ps[:, 0:1], scalar=scale_pm[:, 1:2], in1=beta_f[:],
                                       op0=ALU.mult, op1=ALU.add)

        res = {}
        for n in order:
            b = n // PAIRS_PER_B
            col = (n % PAIRS_PER_B) * 2 * V
            second = n % 2
            if not second:
                res[n // 2] = rpool.tile([P, 4 * V], F32, name="res%d" % (n // 2), tag="res")
            part = res[n // 2][:, second * 2 * V:(second + 1) * 2 * V]
            nc.vector.scalar_tensor_tensor(out=part, in0=y_ps[n][:], scalar=scale_pm[:, 0:1],
                                           in1=x_sb[b][:, col:col + 2 * V], op0=ALU.mult, op1=ALU.add)
            nc.scalar.activation(out=part, in_=part, func=ACT.Relu, bias=shift[:, 0:1], scale=1.0)
            if second:
                nc.sync.dma_start(out=ov[b, :, col - 2 * V:col + 2 * V], in_=res[n // 2][:])
            free.append(bank_of[n])
            multiply_again()
